import numpy as np
import ml_dtypes


def mxq(x, axis, fmt="e4m3"):
    dtype, down = {"e4m3": (ml_dtypes.float8_e4m3fn, 7), "e5m2": (ml_dtypes.float8_e5m2, 14)}[fmt]
    v = np.moveaxis(np.asarray(x, np.float32).astype(ml_dtypes.bfloat16).astype(np.float64), axis, -1)
    blocks = v.reshape(v.shape[:-1] + (-1, 32))
    amax = np.abs(blocks).max(-1, keepdims=True)
    byte = np.maximum(np.where(amax > 0, np.frexp(amax)[1] - 1 + 127, 0) - down, 1)
    scale = np.exp2(byte - 127.0)
    codes = (blocks / scale).astype(np.float32).astype(dtype).astype(np.float64)
    return np.moveaxis((codes * scale).reshape(v.shape), -1, axis)


WIDE = False


def mx_kscale(k):
    if not WIDE:
        return np.ones(k)
    levels = np.array([10, -10, 5, -5, 0])
    if k % 512:
        return np.exp2(np.random.permutation(np.resize(levels, k // 32))).repeat(32)
    a = np.empty((k // 512, 16))
    for p in range(k // 512):
        a[p, :8] = np.random.permutation(np.resize(levels, 8))
        for g in range(8):
            far = levels[np.abs(levels - a[p, g]) >= 10]
            a[p, g + 8] = far[np.random.randint(len(far))]
    return np.exp2(a.ravel()).repeat(32)


BF16 = ml_dtypes.bfloat16


def bf(x):
    return np.asarray(x, np.float32).astype(BF16)


def f64(x):
    return np.asarray(x).astype(np.float64)


N, IN_F, OUT_F = 1024, 512, 512
POW = 2


def setup_inputs():
    s = mx_kscale(IN_F)
    u = np.exp2(np.round(np.log2(mx_kscale(N)) / 2))
    return {"input": bf(np.random.standard_normal((N, IN_F)) * s / (u * u)[:, None]),
            "adj": bf(np.random.uniform(0.0, 1.0, (N, N)) * 1.5 / N ** 0.25 * u),
            "weight": bf(np.random.uniform(-1.0, 1.0, (IN_F, OUT_F)) * 1.7 / np.sqrt(IN_F) / s[:, None]),
            "bias": bf(np.random.standard_normal(OUT_F) * 0.3)}


def reference(input, adj, weight, bias):
    k_adj = f64(adj) ** POW
    support = mxq(f64(input), 1, "e4m3") @ mxq(f64(weight), 0, "e4m3")
    out = (mxq(k_adj, 1, "e4m3") @ mxq(support, 0, "e4m3")) + f64(bias)
    return np.where(out > 0, out, np.expm1(out))

@@ -1,0 +1,246 @@
+from contextlib import ExitStack
+
+import concourse.mybir as mybir
+from concourse.masks import make_identity
+
+NODES, IN_F, OUT_F = 1024, 512, 512
+FLOPS = 2 * NODES * IN_F * OUT_F + 2 * NODES * NODES * OUT_F
+
+F32 = mybir.dt.float32
+BF16 = mybir.dt.bfloat16
+U32 = mybir.dt.uint32
+U8 = mybir.dt.uint8
+FP8X4 = mybir.dt.float8_e4m3fn_x4
+ACT = mybir.ActivationFunctionType
+ALU = mybir.AluOpType
+
+P = 128
+BANK_DT = F32
+
+
+def tile_netgraphconvolution_kernel(tc, x_in, adj, weight, bias, out):
+    nc = tc.nc
+    with ExitStack() as ctx:
+        keep = ctx.enter_context(tc.tile_pool(name="keep", bufs=1))
+        psum = ctx.enter_context(tc.psum_pool(name="psum", bufs=8))
+
+        def sb(name, shape, dtype):
+            return keep.tile(shape, dtype, name=name, align_bytes=64)
+
+        def bank(name, dtype=F32):
+            return psum.tile([P, 512], dtype, name=name, tag="bank")
+
+        x_v = x_in.rearrange("(g m t) f -> g m t f", g=2, t=4)
+        w_v = weight.rearrange("(p j) o -> p j o", j=4)
+        a_v = adj.rearrange("(p r) j -> p r j", r=8)
+        o_v = out.rearrange("(p r) o -> p r o", r=8)
+
+        ident = sb("ident", [P, P], F32)
+        ones = sb("ones", [P, P], BF16)
+        bias_row = sb("bias_row", [P, OUT_F], BF16)
+        bias_sb = sb("bias_sb", [P, OUT_F], F32)
+        warm = sb("warm", [P, 1], F32)
+        w_raw = sb("w_raw", [P, 4, OUT_F], BF16)
+        w_grp = sb("w_grp", [P, OUT_F, 4], BF16)
+        w_cod = sb("w_cod", [P, OUT_F], U32)
+        w_scl = sb("w_scl", [P, OUT_F], U8)
+        x_raw = [sb("x_raw%d" % g, [P, 4, IN_F], BF16) for g in range(2)]
+        x_grp = [sb("x_grp%d" % g, [P, 2048], BF16) for g in range(2)]
+        x_cod = [sb("x_cod%d" % g, [P, 512], U32) for g in range(2)]
+        x_scl = [sb("x_scl%d" % g, [P, 512], U8) for g in range(2)]
+        s_raw = [sb("s_raw%d" % g, [P, 4, OUT_F], BF16) for g in range(2)]
+        s_grp = [sb("s_grp%d" % g, [P, OUT_F, 4], BF16) for g in range(2)]
+        s_cod = [sb("s_cod%d" % g, [P, OUT_F], U32) for g in range(2)]
+        s_scl = [sb("s_scl%d" % g, [P, OUT_F], U8) for g in range(2)]
+        a_raw = [sb("a_raw%d" % c, [P, 2, NODES], BF16) for c in range(4)]
+        a_grp = [sb("a_grp%d" % r, [P, NODES], BF16) for r in range(8)]
+        a_cod = [sb("a_cod%d" % r, [P, 256], U32) for r in range(8)]
+        a_scl = [sb("a_scl%d" % r, [P, 256], U8) for r in range(8)]
+        v_sb = [sb("v_sb%d" % r, [P, OUT_F], F32) for r in range(8)]
+        e_sb = [sb("e_sb%d" % r, [P, OUT_F], F32) for r in range(8)]
+        r_sb = [sb("r_sb%d" % r, [P, OUT_F], F32) for r in range(8)]
+        o_sb = [sb("o_sb%d" % r, [P, OUT_F], F32) for r in range(8)]
+        live = {}
+
+        def head():
+            nc.vector.memset(bias_row[:], 0.0)
+            nc.vector.memset(warm[:], 0.0)
+            nc.sync.dma_start(out=bias_row[0:1, :], in_=bias.rearrange("(a o) -> a o", a=1))
+            nc.sync.dma_start(out=w_raw[:], in_=w_v)
+            for g in range(2):
+                for h in range(2):
+                    nc.sync.dma_start(out=x_raw[g][:, 2 * h : 2 * h + 2, :], in_=x_v[g][:, 2 * h : 2 * h + 2, :])
+            for c in range(4):
+                nc.sync.dma_start(out=a_raw[c][:], in_=a_v[:, 2 * c : 2 * c + 2, :])
+            nc.scalar.activation(out=warm[:], in_=warm[:], func=ACT.Exp)
+            make_identity(nc, ident[:])
+            nc.gpsimd.memset(ones[:], 1.0)
+
+        def bias_mm():
+            b_ps = bank("b_ps")
+            live["b"] = b_ps
+            nc.tensor.matmul(out=b_ps[:], lhsT=ones[:], rhs=bias_row[:], start=True, stop=True)
+
+        def bias_cp(eng):
+            if eng == "S":
+                nc.scalar.copy(out=bias_sb[:], in_=live["b"][:])
+            else:
+                nc.vector.tensor_copy(out=bias_sb[:], in_=live["b"][:])
+
+        def w_interleave(h):
+            cols = slice(256 * h, 256 * (h + 1))
+            nc.vector.tensor_copy(
+                out=w_grp[:, cols, :].rearrange("p (c i) j -> p c j i", i=4),
+                in_=w_raw[:, :, cols].rearrange("p j (c i) -> p c j i", i=4),
+            )
+
+        def w_quant():
+            nc.vector.quantize_mx(out=w_cod[:].bitcast(FP8X4), scales=w_scl[:], in_=w_grp[:].rearrange("p o j -> p (o j)"))
+
+        def x_transpose(g, b):
+            words = x_raw[g][:].rearrange("p t f -> p (t f)").bitcast(F32)
+            xt = bank("xt%d%d" % (g, b))
+            live["xt", g, b] = xt
+            xt4 = xt[:].rearrange("p (u t m) -> p u t m", u=2, t=2)
+            for t2 in range(2):
+                for u in range(2):
+                    t = 2 * b + t2
+                    nc.tensor.transpose(xt4[:, u, t2, :], words[:, 256 * t + u : 256 * (t + 1) : 2], ident[:])
+
+        def x_out(g, b, eng):
+            dst = x_grp[g][:].bitcast(F32)[:, 512 * b : 512 * (b + 1)].rearrange("p (r u) -> p r u", u=2)
+            src = live["xt", g, b][:].rearrange("p (u r) -> p r u", u=2)
+            if eng == "S":
+                nc.scalar.copy(out=dst, in_=src)
+            else:
+                nc.vector.tensor_copy(out=dst, in_=src)
+
+        def x_quant(g):
+            nc.vector.quantize_mx(out=x_cod[g][:].bitcast(FP8X4), scales=x_scl[g][:], in_=x_grp[g][:])
+
+        def mm1(g, t):
+            s_ps = bank("s_ps%d%d" % (g, t), BANK_DT)
+            live["s", g, t] = s_ps
+            cols = slice(P * t, P * (t + 1))
+            nc.tensor.matmul_mx(
+                out=s_ps[:],
+                lhsT=x_cod[g][:, cols].bitcast(FP8X4),
+                lhsT_scale=x_scl[g][:, cols],
+                rhs=w_cod[:].bitcast(FP8X4),
+                rhs_scale=w_scl[:],
+                start=True,
+                stop=True,
+            )
+
+        def s_out(g, t, eng):
+            if eng == "S":
+                nc.scalar.copy(out=s_raw[g][:, t, :], in_=live["s", g, t][:])
+            else:
+                nc.vector.tensor_copy(out=s_raw[g][:, t, :], in_=live["s", g, t][:])
+
+        def s_interleave(g, h):
+            cols = slice(256 * h, 256 * (h + 1))
+            nc.vector.tensor_copy(
+                out=s_grp[g][:, cols, :].rearrange("p (c i) t -> p c t i", i=4),
+                in_=s_raw[g][:, :, cols].rearrange("p t (c i) -> p c t i", i=4),
+            )
+
+        def s_quant(g, h):
+            cols = slice(256 * h, 256 * (h + 1))
+            nc.vector.quantize_mx(out=s_cod[g][:, cols].bitcast(FP8X4), scales=s_scl[g][:, cols], in_=s_grp[g][:, cols, :].rearrange("p o t -> p (o t)"))
+
+        def a_transpose(r):
+            words = a_raw[r // 2][:, r % 2, :].bitcast(F32)
+            at = bank("at%d" % r)
+            live["at", r] = at
+            at4 = at[:].rearrange("p (u g m) -> p u g m", u=2, g=2)
+            for g in range(2):
+                for u in range(2):
+                    nc.tensor.transpose(at4[:, u, g, :], words[:, 256 * g + u : 256 * (g + 1) : 2], ident[:])
+
+        def a_square_out(r):
+            src = live["at", r][:].bitcast(BF16).rearrange("p (u q e) -> p q u e", u=2, e=2)
+            dst = a_grp[r][:].rearrange("p (q u e) -> p q u e", u=2, e=2)
+            nc.scalar.activation(out=dst, in_=src, func=ACT.Square)
+
+        def a_quant(r):
+            nc.vector.quantize_mx(out=a_cod[r][:].bitcast(FP8X4), scales=a_scl[r][:], in_=a_grp[r][:])
+
+        def mm2(r):
+            o_ps = bank("o_ps%d" % r)
+            live["o", r] = o_ps
+            for g in range(2):
+                cols = slice(P * g, P * (g + 1))
+                nc.tensor.matmul_mx(
+                    out=o_ps[:],
+                    lhsT=a_cod[r][:, cols].bitcast(FP8X4),
+                    lhsT_scale=a_scl[r][:, cols],
+                    rhs=s_cod[g][:].bitcast(FP8X4),
+                    rhs_scale=s_scl[g][:],
+                    start=(g == 0),
+                    stop=(g == 1),
+                )
+
+        def ep_add(r):
+            nc.vector.tensor_tensor(out=v_sb[r][:], in0=live["o", r][:], in1=bias_sb[:], op=ALU.add)
+
+        def ep_relu(r, eng):
+            if eng == "S":
+                nc.scalar.activation(out=r_sb[r][:], in_=v_sb[r][:], func=ACT.Relu)
+            else:
+                nc.vector.tensor_scalar_max(out=r_sb[r][:], in0=v_sb[r][:], scalar1=0.0)
+
+        def ep_exp(r):
+            nc.scalar.activation(out=e_sb[r][:], in_=v_sb[r][:], func=ACT.Exp)
+
+        def ep_fin(r):
+            nc.vector.scalar_tensor_tensor(out=o_sb[r][:], in0=e_sb[r][:], scalar=-1.0, in1=r_sb[r][:], op0=ALU.add, op1=ALU.min)
+            nc.sync.dma_start(out=o_v[:, r, :], in_=o_sb[r][:])
+
+        with tc.manual_schedule():
+            head()
+            bias_mm()
+            bias_cp("V")
+            w_interleave(0)
+            w_interleave(1)
+            w_quant()
+            for g in range(2):
+                x_transpose(g, 0)
+                x_transpose(g, 1)
+                x_out(g, 0, "S")
+                x_out(g, 1, "V")
+                x_quant(g)
+            a_transpose(0)
+            a_square_out(0)
+            for g in range(2):
+                for t in range(4):
+                    mm1(g, t)
+            for t in range(4):
+                s_out(0, t, "S" if t < 1 else "V")
+            for t in range(4):
+                s_out(1, t, "S")
+            a_quant(0)
+            for r in range(1, 8):
+                a_transpose(r)
+            for g in range(2):
+                for h in range(2):
+                    s_interleave(g, h)
+            for g in range(2):
+                for h in range(2):
+                    s_quant(g, h)
+            for r in range(1, 4):
+                a_square_out(r)
+                a_quant(r)
+            for r in range(8 + 2):
+                if r < 8:
+                    mm2(r)
+                    if r + 4 < 8:
+                        a_square_out(r + 4)
+                    ep_add(r)
+                    ep_exp(r)
+                if r >= 2:
+                    ep_fin(r - 2)
+                if r < 8:
+                    ep_relu(r, "S" if 3 <= r < 7 else "V")
+                    if r + 4 < 8:
+                        a_quant(r + 4)

@@ -40,6 +40,7 @@ def tile_netgraphconvolution_kernel(tc, x_in, adj, weight, bias, out):
         bias_row = sb("bias_row", [P, OUT_F], BF16)
         bias_sb = sb("bias_sb", [P, OUT_F], F32)
         warm = sb("warm", [P, 1], F32)
+        dmy = sb("dmy", [P, P], F32)
         w_raw = sb("w_raw", [P, 4, OUT_F], BF16)
         w_grp = sb("w_grp", [P, OUT_F, 4], BF16)
         w_cod = sb("w_cod", [P, OUT_F], U32)
@@ -63,18 +64,24 @@ def tile_netgraphconvolution_kernel(tc, x_in, adj, weight, bias, out):
         live = {}
 
         def head():
-            nc.vector.memset(bias_row[:], 0.0)
+            nc.vector.memset(dmy[:], 0.0)
             nc.vector.memset(warm[:], 0.0)
-            nc.sync.dma_start(out=bias_row[0:1, :], in_=bias.rearrange("(a o) -> a o", a=1))
+            nc.vector.memset(bias_row[:], 0.0)
             nc.sync.dma_start(out=w_raw[:], in_=w_v)
-            for g in range(2):
-                for h in range(2):
-                    nc.sync.dma_start(out=x_raw[g][:, 2 * h : 2 * h + 2, :], in_=x_v[g][:, 2 * h : 2 * h + 2, :])
+            for h in range(2):
+                nc.sync.dma_start(out=x_raw[0][:, 2 * h : 2 * h + 2, :], in_=x_v[0][:, 2 * h : 2 * h + 2, :])
+            nc.sync.dma_start(out=bias_row[0:1, :], in_=bias.rearrange("(a o) -> a o", a=1))
+            for h in range(2):
+                nc.sync.dma_start(out=x_raw[1][:, 2 * h : 2 * h + 2, :], in_=x_v[1][:, 2 * h : 2 * h + 2, :])
             for c in range(4):
                 nc.sync.dma_start(out=a_raw[c][:], in_=a_v[:, 2 * c : 2 * c + 2, :])
             nc.scalar.activation(out=warm[:], in_=warm[:], func=ACT.Exp)
             make_identity(nc, ident[:])
             nc.gpsimd.memset(ones[:], 1.0)
+
+        def keep_warm(tile, n):
+            for k in range(n):
+                nc.tensor.matmul(out=tile[:, 0:P], lhsT=dmy[:], rhs=dmy[:], start=True, stop=True)
 
         def bias_mm():
             b_ps = bank("b_ps")
@@ -97,10 +104,11 @@ def tile_netgraphconvolution_kernel(tc, x_in, adj, weight, bias, out):
         def w_quant():
             nc.vector.quantize_mx(out=w_cod[:].bitcast(FP8X4), scales=w_scl[:], in_=w_grp[:].rearrange("p o j -> p (o j)"))
 
-        def x_transpose(g, b):
+        def x_transpose(g, b, n_warm):
             words = x_raw[g][:].rearrange("p t f -> p (t f)").bitcast(F32)
             xt = bank("xt%d%d" % (g, b))
             live["xt", g, b] = xt
+            keep_warm(xt, n_warm)
             xt4 = xt[:].rearrange("p (u t m) -> p u t m", u=2, t=2)
             for t2 in range(2):
                 for u in range(2):
@@ -149,10 +157,11 @@ def tile_netgraphconvolution_kernel(tc, x_in, adj, weight, bias, out):
             cols = slice(256 * h, 256 * (h + 1))
             nc.vector.quantize_mx(out=s_cod[g][:, cols].bitcast(FP8X4), scales=s_scl[g][:, cols], in_=s_grp[g][:, cols, :].rearrange("p o t -> p (o t)"))
 
-        def a_transpose(r):
+        def a_transpose(r, n_warm):
             words = a_raw[r // 2][:, r % 2, :].bitcast(F32)
             at = bank("at%d" % r)
             live["at", r] = at
+            keep_warm(at, n_warm)
             at4 = at[:].rearrange("p (u g m) -> p u g m", u=2, g=2)
             for g in range(2):
                 for u in range(2):
@@ -199,18 +208,19 @@ def tile_netgraphconvolution_kernel(tc, x_in, adj, weight, bias, out):
 
         with tc.manual_schedule():
             head()
-            bias_mm()
-            bias_cp("V")
             w_interleave(0)
             w_interleave(1)
-            w_quant()
             for g in range(2):
-                x_transpose(g, 0)
-                x_transpose(g, 1)
-                x_out(g, 0, "S")
-                x_out(g, 1, "V")
+                x_transpose(g, 0, 8 if g == 0 else 1)
+                x_transpose(g, 1, 1)
+                x_out(g, 0, "V")
+                if g == 0:
+                    w_quant()
+                x_out(g, 1, "S")
                 x_quant(g)
-            a_transpose(0)
+            bias_mm()
+            bias_cp("S")
+            a_transpose(0, 1)
             a_square_out(0)
             for g in range(2):
                 for t in range(4):
@@ -220,8 +230,8 @@ def tile_netgraphconvolution_kernel(tc, x_in, adj, weight, bias, out):
             for t in range(4):
                 s_out(1, t, "S")
             a_quant(0)
-            for r in range(1, 8):
-                a_transpose(r)
+            for r in range(1, 6):
+                a_transpose(r, 1)
             for g in range(2):
                 for h in range(2):
                     s_interleave(g, h)
@@ -234,6 +244,8 @@ def tile_netgraphconvolution_kernel(tc, x_in, adj, weight, bias, out):
             for r in range(8 + 2):
                 if r < 8:
                     mm2(r)
+                    if 6 <= r + 6 - 1 < 8 and r >= 1:
+                        a_transpose(r + 6 - 1, 0)
                     if r + 4 < 8:
                         a_square_out(r + 4)
                     ep_add(r)

@@ -96,10 +96,7 @@ def tile_netgraphconvolution_kernel(tc, x_in, adj, weight, bias, out):
 
         def w_interleave(h):
             cols = slice(256 * h, 256 * (h + 1))
-            nc.vector.tensor_copy(
-                out=w_grp[:, cols, :].rearrange("p (c i) j -> p c j i", i=4),
-                in_=w_raw[:, :, cols].rearrange("p j (c i) -> p c j i", i=4),
-            )
+            nc.vector.tensor_copy(out=w_grp[:, cols, :], in_=w_raw[:, :, cols].rearrange("p j o -> p o j"))
 
         def w_quant():
             nc.vector.quantize_mx(out=w_cod[:].bitcast(FP8X4), scales=w_scl[:], in_=w_grp[:].rearrange("p o j -> p (o j)"))
@@ -148,10 +145,7 @@ def tile_netgraphconvolution_kernel(tc, x_in, adj, weight, bias, out):
 
         def s_interleave(g, h):
             cols = slice(256 * h, 256 * (h + 1))
-            nc.vector.tensor_copy(
-                out=s_grp[g][:, cols, :].rearrange("p (c i) t -> p c t i", i=4),
-                in_=s_raw[g][:, :, cols].rearrange("p t (c i) -> p c t i", i=4),
-            )
+            nc.vector.tensor_copy(out=s_grp[g][:, cols, :], in_=s_raw[g][:, :, cols].rearrange("p t o -> p o t"))
 
         def s_quant(g, h):
             cols = slice(256 * h, 256 * (h + 1))

from contextlib import ExitStack

import concourse.mybir as mybir
from concourse.masks import make_identity

NODES, IN_F, OUT_F = 1024, 512, 512
FLOPS = 2 * NODES * IN_F * OUT_F + 2 * NODES * NODES * OUT_F

F32 = mybir.dt.float32
BF16 = mybir.dt.bfloat16
U32 = mybir.dt.uint32
U8 = mybir.dt.uint8
FP8X4 = mybir.dt.float8_e4m3fn_x4
ACT = mybir.ActivationFunctionType
ALU = mybir.AluOpType

P = 128
BANK_DT = F32


def tile_netgraphconvolution_kernel(tc, x_in, adj, weight, bias, out):
    nc = tc.nc
    with ExitStack() as ctx:
        keep = ctx.enter_context(tc.tile_pool(name="keep", bufs=1))
        psum = ctx.enter_context(tc.psum_pool(name="psum", bufs=8))

        def sb(name, shape, dtype):
            return keep.tile(shape, dtype, name=name, align_bytes=64)

        def bank(name, dtype=F32):
            return psum.tile([P, 512], dtype, name=name, tag="bank")

        x_v = x_in.rearrange("(g m t) f -> g m t f", g=2, t=4)
        w_v = weight.rearrange("(p j) o -> p j o", j=4)
        a_v = adj.rearrange("(p r) j -> p r j", r=8)
        o_v = out.rearrange("(p r) o -> p r o", r=8)

        ident = sb("ident", [P, P], F32)
        ones = sb("ones", [P, P], BF16)
        bias_row = sb("bias_row", [P, OUT_F], BF16)
        bias_sb = sb("bias_sb", [P, OUT_F], F32)
        warm = sb("warm", [P, 1], F32)
        dmy = sb("dmy", [P, P], F32)
        w_raw = sb("w_raw", [P, 4, OUT_F], BF16)
        w_grp = sb("w_grp", [P, OUT_F, 4], BF16)
        w_cod = sb("w_cod", [P, OUT_F], U32)
        w_scl = sb("w_scl", [P, OUT_F], U8)
        x_raw = [sb("x_raw%d" % g, [P, 4, IN_F], BF16) for g in range(2)]
        x_grp = [sb("x_grp%d" % g, [P, 2048], BF16) for g in range(2)]
        x_cod = [sb("x_cod%d" % g, [P, 512], U32) for g in range(2)]
        x_scl = [sb("x_scl%d" % g, [P, 512], U8) for g in range(2)]
        s_raw = [sb("s_raw%d" % g, [P, 4, OUT_F], BF16) for g in range(2)]
        s_grp = [sb("s_grp%d" % g, [P, OUT_F, 4], BF16) for g in range(2)]
        s_cod = [sb("s_cod%d" % g, [P, OUT_F], U32) for g in range(2)]
        s_scl = [sb("s_scl%d" % g, [P, OUT_F], U8) for g in range(2)]
        a_raw = [sb("a_raw%d" % c, [P, 2, NODES], BF16) for c in range(4)]
        a_grp = [sb("a_grp%d" % r, [P, NODES], BF16) for r in range(8)]
        a_cod = [sb("a_cod%d" % r, [P, 256], U32) for r in range(8)]
        a_scl = [sb("a_scl%d" % r, [P, 256], U8) for r in range(8)]
        v_sb = [sb("v_sb%d" % r, [P, OUT_F], F32) for r in range(8)]
        e_sb = [sb("e_sb%d" % r, [P, OUT_F], F32) for r in range(8)]
        r_sb = [sb("r_sb%d" % r, [P, OUT_F], F32) for r in range(8)]
        o_sb = [sb("o_sb%d" % r, [P, OUT_F], F32) for r in range(8)]
        live = {}

        def head():
            nc.vector.memset(dmy[:], 0.0)
            nc.vector.memset(warm[:], 0.0)
            nc.vector.memset(bias_row[:], 0.0)
            nc.sync.dma_start(out=w_raw[:], in_=w_v)
            for h in range(2):
                nc.sync.dma_start(out=x_raw[0][:, 2 * h : 2 * h + 2, :], in_=x_v[0][:, 2 * h : 2 * h + 2, :])
            nc.sync.dma_start(out=bias_row[0:1, :], in_=bias.rearrange("(a o) -> a o", a=1))
            for h in range(2):
                nc.sync.dma_start(out=x_raw[1][:, 2 * h : 2 * h + 2, :], in_=x_v[1][:, 2 * h : 2 * h + 2, :])
            for c in range(4):
                nc.sync.dma_start(out=a_raw[c][:], in_=a_v[:, 2 * c : 2 * c + 2, :])
            nc.scalar.activation(out=warm[:], in_=warm[:], func=ACT.Exp)
            make_identity(nc, ident[:])
            nc.gpsimd.memset(ones[:], 1.0)

        def keep_warm(tile, n):
            for k in range(n):
                nc.tensor.matmul(out=tile[:, 0:P], lhsT=dmy[:], rhs=dmy[:], start=True, stop=True)

        def bias_mm():
            b_ps = bank("b_ps")
            live["b"] = b_ps
            nc.tensor.matmul(out=b_ps[:], lhsT=ones[:], rhs=bias_row[:], start=True, stop=True)

        def bias_cp(eng):
            if eng == "S":
                nc.scalar.copy(out=bias_sb[:], in_=live["b"][:])
            else:
                nc.vector.tensor_copy(out=bias_sb[:], in_=live["b"][:])

        def w_interleave(h):
            cols = slice(256 * h, 256 * (h + 1))
            nc.vector.tensor_copy(out=w_grp[:, cols, :], in_=w_raw[:, :, cols].rearrange("p j o -> p o j"))

        def w_quant():
            nc.vector.quantize_mx(out=w_cod[:].bitcast(FP8X4), scales=w_scl[:], in_=w_grp[:].rearrange("p o j -> p (o j)"))

        def x_transpose(g, b, n_warm):
            words = x_raw[g][:].rearrange("p t f -> p (t f)").bitcast(F32)
            xt = bank("xt%d%d" % (g, b))
            live["xt", g, b] = xt
            keep_warm(xt, n_warm)
            xt4 = xt[:].rearrange("p (u t m) -> p u t m", u=2, t=2)
            for t2 in range(2):
                for u in range(2):
                    t = 2 * b + t2
                    nc.tensor.transpose(xt4[:, u, t2, :], words[:, 256 * t + u : 256 * (t + 1) : 2], ident[:])

        def x_out(g, b, eng):
            dst = x_grp[g][:].bitcast(F32)[:, 512 * b : 512 * (b + 1)].rearrange("p (r u) -> p r u", u=2)
            src = live["xt", g, b][:].rearrange("p (u r) -> p r u", u=2)
            if eng == "S":
                nc.scalar.copy(out=dst, in_=src)
            else:
                nc.vector.tensor_copy(out=dst, in_=src)

        def x_quant(g):
            nc.vector.quantize_mx(out=x_cod[g][:].bitcast(FP8X4), scales=x_scl[g][:], in_=x_grp[g][:])

        def mm1(g, t):
            s_ps = bank("s_ps%d%d" % (g, t), BANK_DT)
            live["s", g, t] = s_ps
            cols = slice(P * t, P * (t + 1))
            nc.tensor.matmul_mx(
                out=s_ps[:],
                lhsT=x_cod[g][:, cols].bitcast(FP8X4),
                lhsT_scale=x_scl[g][:, cols],
                rhs=w_cod[:].bitcast(FP8X4),
                rhs_scale=w_scl[:],
                start=True,
                stop=True,
            )

        def s_out(g, t, eng):
            if eng == "S":
                nc.scalar.copy(out=s_raw[g][:, t, :], in_=live["s", g, t][:])
            else:
                nc.vector.tensor_copy(out=s_raw[g][:, t, :], in_=live["s", g, t][:])

        def s_interleave(g, h):
            cols = slice(256 * h, 256 * (h + 1))
            nc.vector.tensor_copy(out=s_grp[g][:, cols, :], in_=s_raw[g][:, :, cols].rearrange("p t o -> p o t"))

        def s_quant(g, h):
            cols = slice(256 * h, 256 * (h + 1))
            nc.vector.quantize_mx(out=s_cod[g][:, cols].bitcast(FP8X4), scales=s_scl[g][:, cols], in_=s_grp[g][:, cols, :].rearrange("p o t -> p (o t)"))

        def a_transpose(r, n_warm):
            words = a_raw[r // 2][:, r % 2, :].bitcast(F32)
            at = bank("at%d" % r)
            live["at", r] = at
            keep_warm(at, n_warm)
            at4 = at[:].rearrange("p (u g m) -> p u g m", u=2, g=2)
            for g in range(2):
                for u in range(2):
                    nc.tensor.transpose(at4[:, u, g, :], words[:, 256 * g + u : 256 * (g + 1) : 2], ident[:])

        def a_square_out(r):
            src = live["at", r][:].bitcast(BF16).rearrange("p (u q e) -> p q u e", u=2, e=2)
            dst = a_grp[r][:].rearrange("p (q u e) -> p q u e", u=2, e=2)
            nc.scalar.activation(out=dst, in_=src, func=ACT.Square)

        def a_quant(r):
            nc.vector.quantize_mx(out=a_cod[r][:].bitcast(FP8X4), scales=a_scl[r][:], in_=a_grp[r][:])

        def mm2(r):
            o_ps = bank("o_ps%d" % r)
            live["o", r] = o_ps
            for g in range(2):
                cols = slice(P * g, P * (g + 1))
                nc.tensor.matmul_mx(
                    out=o_ps[:],
                    lhsT=a_cod[r][:, cols].bitcast(FP8X4),
                    lhsT_scale=a_scl[r][:, cols],
                    rhs=s_cod[g][:].bitcast(FP8X4),
                    rhs_scale=s_scl[g][:],
                    start=(g == 0),
                    stop=(g == 1),
                )

        def ep_add(r):
            nc.vector.tensor_tensor(out=v_sb[r][:], in0=live["o", r][:], in1=bias_sb[:], op=ALU.add)

        def ep_relu(r, eng):
            if eng == "S":
                nc.scalar.activation(out=r_sb[r][:], in_=v_sb[r][:], func=ACT.Relu)
            else:
                nc.vector.tensor_scalar_max(out=r_sb[r][:], in0=v_sb[r][:], scalar1=0.0)

        def ep_exp(r):
            nc.scalar.activation(out=e_sb[r][:], in_=v_sb[r][:], func=ACT.Exp)

        def ep_fin(r):
            nc.vector.scalar_tensor_tensor(out=o_sb[r][:], in0=e_sb[r][:], scalar=-1.0, in1=r_sb[r][:], op0=ALU.add, op1=ALU.min)
            nc.sync.dma_start(out=o_v[:, r, :], in_=o_sb[r][:])

        with tc.manual_schedule():
            head()
            w_interleave(0)
            w_interleave(1)
            for g in range(2):
                x_transpose(g, 0, 8 if g == 0 else 1)
                x_transpose(g, 1, 1)
                x_out(g, 0, "V")
                if g == 0:
                    w_quant()
                x_out(g, 1, "S")
                x_quant(g)
            bias_mm()
            bias_cp("S")
            a_transpose(0, 1)
            a_square_out(0)
            for g in range(2):
                for t in range(4):
                    mm1(g, t)
            for t in range(4):
                s_out(0, t, "S" if t < 1 else "V")
            for t in range(4):
                s_out(1, t, "S")
            a_quant(0)
            for r in range(1, 6):
                a_transpose(r, 1)
            for g in range(2):
                for h in range(2):
                    s_interleave(g, h)
            for g in range(2):
                for h in range(2):
                    s_quant(g, h)
            for r in range(1, 4):
                a_square_out(r)
                a_quant(r)
            for r in range(8 + 2):
                if r < 8:
                    mm2(r)
                    if 6 <= r + 6 - 1 < 8 and r >= 1:
                        a_transpose(r + 6 - 1, 0)
                    if r + 4 < 8:
                        a_square_out(r + 4)
                    ep_add(r)
                    ep_exp(r)
                if r >= 2:
                    ep_fin(r - 2)
                if r < 8:
                    ep_relu(r, "S" if 3 <= r < 7 else "V")
                    if r + 4 < 8:
                        a_quant(r + 4)
